import numpy as np
import ml_dtypes

BF16 = ml_dtypes.bfloat16


def bf(x):
    return np.asarray(x, np.float32).astype(BF16)


def f32(x):
    return np.asarray(x, np.float32)


def f64(x):
    return np.asarray(x).astype(np.float64)


def striped(idx):
    return np.tile(idx.reshape(-1, 16).T, (8, 1))


S, D, M, N, HQ, HKV = 512, 128, 256, 64, 4, 2
HALF = D // 2
NH = HQ + HKV
BASE = 10000.0


def spread():
    w = np.zeros((D, M))
    m = np.arange(D)
    w[m % HALF, m] = 1.0
    w[HALF + m % HALF, D + m] = np.where(m < HALF, -1.0, 1.0)
    return w


def setup_inputs():
    inv_freq = 1.0 / BASE ** (np.arange(HALF) / HALF)
    ang = np.outer(np.arange(S), inv_freq)
    return {"table": bf(np.concatenate([np.cos(ang), np.sin(ang)], axis=1)), "w": bf(spread()), "x": f32(np.random.standard_normal((NH * D, N))), "offs": striped(np.random.permutation(np.tile(np.arange(S), 2))[:N])}


def reference(table, w, x, offs):
    idx = offs[:16].T.reshape(-1)
    cs = f64(w).T @ f64(table)[idx].T
    c, s = cs[:D], cs[D:]
    xv = f64(x).reshape(NH, D, N)
    xr = np.concatenate([xv[:, HALF:], xv[:, :HALF]], axis=1)
    return (xv * c[None] + xr * s[None]).reshape(NH * D, N)

@@ -1,0 +1,65 @@
+import concourse.mybir as mybir
+from concourse.masks import make_identity
+
+P = 128
+S = 512
+N = 64
+NH = 6
+HALF = 64
+BLOCKS = S // P
+
+BF16, F32, U16 = mybir.dt.bfloat16, mybir.dt.float32, mybir.dt.uint16
+MULT, ADD = mybir.AluOpType.mult, mybir.AluOpType.add
+
+FLOPS = 2 * P * 2 * P * N
+
+
+def tile_openpangusinkattention_kernel(tc, table, w, x, offs, out):
+    nc = tc.nc
+    x_heads = x.rearrange("(h e) j -> e h j", e=P)
+    out_heads = out.rearrange("(h e) j -> e h j", e=P)
+    with (
+        tc.tile_pool(name="held", bufs=1) as held,
+        tc.psum_pool(name="psum", bufs=1) as psum,
+    ):
+        offsets = held.tile([P, N // 16], U16, name="offsets")
+        nc.sync.dma_start(offsets[:], offs)
+
+        rows = held.tile([P, BLOCKS, P], BF16, name="rows")
+        nc.sync.dma_start(rows[:], table.rearrange("(b p) d -> p b d", p=P))
+
+        weights = held.tile([P, 2 * P], BF16, name="weights")
+        nc.scalar.dma_start(weights[:], w)
+
+        x_same = held.tile([P, NH, N], F32, name="x_same")
+        nc.scalar.dma_start(x_same[:], x_heads)
+        x_swap = held.tile([P, NH, N], F32, name="x_swap")
+        nc.sync.dma_start(x_swap[0:HALF], x_heads[HALF:P])
+        nc.scalar.dma_start(x_swap[HALF:P], x_heads[0:HALF])
+
+        identity = held.tile([P, P], BF16, name="identity")
+        make_identity(nc, identity[:])
+
+        flipped = psum.tile([P, S], BF16, name="flipped")
+        for b in range(BLOCKS):
+            nc.tensor.transpose(flipped[:, b * P : (b + 1) * P], rows[:, b, :], identity[:])
+        window = held.tile([P, S], BF16, name="window")
+        nc.vector.tensor_copy(window[:], flipped[:])
+
+        cs = psum.tile([P, 2, N], F32, name="cs")
+        for k in range(2):
+            nc.tensor.matmul(
+                cs[:, k, :],
+                weights[:, k * P : (k + 1) * P],
+                window[:].indirect(offsets[:]),
+                start=True,
+                stop=True,
+            )
+
+        by_cos = held.tile([P, NH, N], F32, name="by_cos")
+        by_sin = held.tile([P, NH, N], F32, name="by_sin")
+        rotated = held.tile([P, NH, N], F32, name="rotated")
+        nc.vector.tensor_tensor(by_cos[:], x_same[:], cs[:, 0, :].unsqueeze(1).to_broadcast([P, NH, N]), MULT)
+        nc.vector.tensor_tensor(by_sin[:], x_swap[:], cs[:, 1, :].unsqueeze(1).to_broadcast([P, NH, N]), MULT)
+        nc.vector.tensor_tensor(rotated[:], by_cos[:], by_sin[:], ADD)
+        nc.sync.dma_start(out_heads, rotated[:])

@@ -22,12 +22,13 @@ def tile_openpangusinkattention_kernel(tc, table, w, x, offs, out):
         tc.tile_pool(name="held", bufs=1) as held,
         tc.psum_pool(name="psum", bufs=1) as psum,
     ):
+        rows = [held.tile([P, P], BF16, name=f"rows{b}") for b in range(BLOCKS)]
+        for b in range(BLOCKS):
+            queue = nc.sync if b % 2 == 0 else nc.scalar
+            queue.dma_start(rows[b][:], table[b * P : (b + 1) * P, :])
+
         offsets = held.tile([P, N // 16], U16, name="offsets")
         nc.sync.dma_start(offsets[:], offs)
-
-        rows = held.tile([P, BLOCKS, P], BF16, name="rows")
-        nc.sync.dma_start(rows[:], table.rearrange("(b p) d -> p b d", p=P))
-
         weights = held.tile([P, 2 * P], BF16, name="weights")
         nc.scalar.dma_start(weights[:], w)
 
@@ -35,14 +36,14 @@ def tile_openpangusinkattention_kernel(tc, table, w, x, offs, out):
         nc.scalar.dma_start(x_same[:], x_heads)
         x_swap = held.tile([P, NH, N], F32, name="x_swap")
         nc.sync.dma_start(x_swap[0:HALF], x_heads[HALF:P])
-        nc.scalar.dma_start(x_swap[HALF:P], x_heads[0:HALF])
+        nc.sync.dma_start(x_swap[HALF:P], x_heads[0:HALF])
 
         identity = held.tile([P, P], BF16, name="identity")
         make_identity(nc, identity[:])
 
         flipped = psum.tile([P, S], BF16, name="flipped")
         for b in range(BLOCKS):
-            nc.tensor.transpose(flipped[:, b * P : (b + 1) * P], rows[:, b, :], identity[:])
+            nc.tensor.transpose(flipped[:, b * P : (b + 1) * P], rows[b][:], identity[:])
         window = held.tile([P, S], BF16, name="window")
         nc.vector.tensor_copy(window[:], flipped[:])
 

@@ -41,16 +41,19 @@ def tile_openpangusinkattention_kernel(tc, table, w, x, offs, out):
         identity = held.tile([P, P], BF16, name="identity")
         make_identity(nc, identity[:])
 
-        flipped = psum.tile([P, S], BF16, name="flipped")
-        for b in range(BLOCKS):
-            nc.tensor.transpose(flipped[:, b * P : (b + 1) * P], rows[b][:], identity[:])
         window = held.tile([P, S], BF16, name="window")
-        nc.vector.tensor_copy(window[:], flipped[:])
+        for b in range(BLOCKS):
+            flipped = psum.tile([P, P], BF16, name=f"flipped{b}")
+            nc.tensor.transpose(flipped[:], rows[b][:], identity[:])
+            if b % 2 == 0:
+                nc.vector.tensor_copy(window[:, b * P : (b + 1) * P], flipped[:])
+            else:
+                nc.scalar.copy(window[:, b * P : (b + 1) * P], flipped[:])
 
-        cs = psum.tile([P, 2, N], F32, name="cs")
+        cs = [psum.tile([P, N], F32, name=f"cs{k}") for k in range(2)]
         for k in range(2):
             nc.tensor.matmul(
-                cs[:, k, :],
+                cs[k][:],
                 weights[:, k * P : (k + 1) * P],
                 window[:].indirect(offsets[:]),
                 start=True,
@@ -60,7 +63,7 @@ def tile_openpangusinkattention_kernel(tc, table, w, x, offs, out):
         by_cos = held.tile([P, NH, N], F32, name="by_cos")
         by_sin = held.tile([P, NH, N], F32, name="by_sin")
         rotated = held.tile([P, NH, N], F32, name="rotated")
-        nc.vector.tensor_tensor(by_cos[:], x_same[:], cs[:, 0, :].unsqueeze(1).to_broadcast([P, NH, N]), MULT)
-        nc.vector.tensor_tensor(by_sin[:], x_swap[:], cs[:, 1, :].unsqueeze(1).to_broadcast([P, NH, N]), MULT)
+        nc.vector.tensor_tensor(by_cos[:], x_same[:], cs[0][:].unsqueeze(1).to_broadcast([P, NH, N]), MULT)
+        nc.vector.tensor_tensor(by_sin[:], x_swap[:], cs[1][:].unsqueeze(1).to_broadcast([P, NH, N]), MULT)
         nc.vector.tensor_tensor(rotated[:], by_cos[:], by_sin[:], ADD)
         nc.sync.dma_start(out_heads, rotated[:])

@@ -7,6 +7,8 @@ N = 64
 NH = 6
 HALF = 64
 BLOCKS = S // P
+GROUPS = 2
+GH = NH // GROUPS
 
 BF16, F32, U16 = mybir.dt.bfloat16, mybir.dt.float32, mybir.dt.uint16
 MULT, ADD = mybir.AluOpType.mult, mybir.AluOpType.add
@@ -41,19 +43,16 @@ def tile_openpangusinkattention_kernel(tc, table, w, x, offs, out):
         identity = held.tile([P, P], BF16, name="identity")
         make_identity(nc, identity[:])
 
-        window = held.tile([P, S], BF16, name="window")
+        flipped = psum.tile([P, S], BF16, name="flipped")
         for b in range(BLOCKS):
-            flipped = psum.tile([P, P], BF16, name=f"flipped{b}")
-            nc.tensor.transpose(flipped[:], rows[b][:], identity[:])
-            if b % 2 == 0:
-                nc.vector.tensor_copy(window[:, b * P : (b + 1) * P], flipped[:])
-            else:
-                nc.scalar.copy(window[:, b * P : (b + 1) * P], flipped[:])
+            nc.tensor.transpose(flipped[:, b * P : (b + 1) * P], rows[b][:], identity[:])
+        window = held.tile([P, S], BF16, name="window")
+        nc.vector.tensor_copy(window[:], flipped[:])
 
-        cs = [psum.tile([P, N], F32, name=f"cs{k}") for k in range(2)]
+        cs = psum.tile([P, 2, N], F32, name="cs")
         for k in range(2):
             nc.tensor.matmul(
-                cs[k][:],
+                cs[:, k, :],
                 weights[:, k * P : (k + 1) * P],
                 window[:].indirect(offsets[:]),
                 start=True,
@@ -61,9 +60,14 @@ def tile_openpangusinkattention_kernel(tc, table, w, x, offs, out):
             )
 
         by_cos = held.tile([P, NH, N], F32, name="by_cos")
-        by_sin = held.tile([P, NH, N], F32, name="by_sin")
-        rotated = held.tile([P, NH, N], F32, name="rotated")
-        nc.vector.tensor_tensor(by_cos[:], x_same[:], cs[0][:].unsqueeze(1).to_broadcast([P, NH, N]), MULT)
-        nc.vector.tensor_tensor(by_sin[:], x_swap[:], cs[1][:].unsqueeze(1).to_broadcast([P, NH, N]), MULT)
-        nc.vector.tensor_tensor(rotated[:], by_cos[:], by_sin[:], ADD)
-        nc.sync.dma_start(out_heads, rotated[:])
+        nc.vector.tensor_tensor(by_cos[:], x_same[:], cs[:, 0, :].unsqueeze(1).to_broadcast([P, NH, N]), MULT)
+        for g in range(GROUPS):
+            heads = slice(g * GH, (g + 1) * GH)
+            by_sin = held.tile([P, GH, N], F32, name=f"by_sin{g}")
+            rotated = held.tile([P, GH, N], F32, name=f"rotated{g}")
+            nc.vector.tensor_tensor(
+                by_sin[:], x_swap[:, heads, :], cs[:, 1, :].unsqueeze(1).to_broadcast([P, GH, N]), MULT
+            )
+            nc.vector.tensor_tensor(rotated[:], by_cos[:, heads, :], by_sin[:], ADD)
+            queue = nc.sync if g % 2 == 0 else nc.scalar
+            queue.dma_start(out_heads[:, heads, :], rotated[:])

@@ -34,11 +34,13 @@ def tile_openpangusinkattention_kernel(tc, table, w, x, offs, out):
         weights = held.tile([P, 2 * P], BF16, name="weights")
         nc.scalar.dma_start(weights[:], w)
 
-        x_same = held.tile([P, NH, N], F32, name="x_same")
-        nc.scalar.dma_start(x_same[:], x_heads)
-        x_swap = held.tile([P, NH, N], F32, name="x_swap")
-        nc.sync.dma_start(x_swap[0:HALF], x_heads[HALF:P])
-        nc.sync.dma_start(x_swap[HALF:P], x_heads[0:HALF])
+        x_same = [held.tile([P, GH, N], F32, name=f"x_same{g}") for g in range(GROUPS)]
+        x_swap = [held.tile([P, GH, N], F32, name=f"x_swap{g}") for g in range(GROUPS)]
+        for g in range(GROUPS):
+            heads = slice(g * GH, (g + 1) * GH)
+            nc.scalar.dma_start(x_same[g][:], x_heads[:, heads, :])
+            nc.sync.dma_start(x_swap[g][0:HALF], x_heads[HALF:P, heads, :])
+            nc.sync.dma_start(x_swap[g][HALF:P], x_heads[0:HALF, heads, :])
 
         identity = held.tile([P, P], BF16, name="identity")
         make_identity(nc, identity[:])
@@ -58,16 +60,16 @@ def tile_openpangusinkattention_kernel(tc, table, w, x, offs, out):
                 start=True,
                 stop=True,
             )
+        cos = cs[:, 0, :].unsqueeze(1).to_broadcast([P, GH, N])
+        sin = cs[:, 1, :].unsqueeze(1).to_broadcast([P, GH, N])
 
-        by_cos = held.tile([P, NH, N], F32, name="by_cos")
-        nc.vector.tensor_tensor(by_cos[:], x_same[:], cs[:, 0, :].unsqueeze(1).to_broadcast([P, NH, N]), MULT)
         for g in range(GROUPS):
             heads = slice(g * GH, (g + 1) * GH)
+            by_cos = held.tile([P, GH, N], F32, name=f"by_cos{g}")
             by_sin = held.tile([P, GH, N], F32, name=f"by_sin{g}")
             rotated = held.tile([P, GH, N], F32, name=f"rotated{g}")
-            nc.vector.tensor_tensor(
-                by_sin[:], x_swap[:, heads, :], cs[:, 1, :].unsqueeze(1).to_broadcast([P, GH, N]), MULT
-            )
-            nc.vector.tensor_tensor(rotated[:], by_cos[:, heads, :], by_sin[:], ADD)
+            nc.vector.tensor_tensor(by_cos[:], x_same[g][:], cos, MULT)
+            nc.vector.tensor_tensor(by_sin[:], x_swap[g][:], sin, MULT)
+            nc.vector.tensor_tensor(rotated[:], by_cos[:], by_sin[:], ADD)
             queue = nc.sync if g % 2 == 0 else nc.scalar
             queue.dma_start(out_heads[:, heads, :], rotated[:])

@@ -34,13 +34,12 @@ def tile_openpangusinkattention_kernel(tc, table, w, x, offs, out):
         weights = held.tile([P, 2 * P], BF16, name="weights")
         nc.scalar.dma_start(weights[:], w)
 
-        x_same = [held.tile([P, GH, N], F32, name=f"x_same{g}") for g in range(GROUPS)]
-        x_swap = [held.tile([P, GH, N], F32, name=f"x_swap{g}") for g in range(GROUPS)]
+        x_pair = [held.tile([P, 2, GH, N], F32, name=f"x_pair{g}") for g in range(GROUPS)]
         for g in range(GROUPS):
             heads = slice(g * GH, (g + 1) * GH)
-            nc.scalar.dma_start(x_same[g][:], x_heads[:, heads, :])
-            nc.sync.dma_start(x_swap[g][0:HALF], x_heads[HALF:P, heads, :])
-            nc.sync.dma_start(x_swap[g][HALF:P], x_heads[0:HALF, heads, :])
+            nc.scalar.dma_start(x_pair[g][:, 0], x_heads[:, heads, :])
+            nc.sync.dma_start(x_pair[g][0:HALF, 1], x_heads[HALF:P, heads, :])
+            nc.sync.dma_start(x_pair[g][HALF:P, 1], x_heads[0:HALF, heads, :])
 
         identity = held.tile([P, P], BF16, name="identity")
         make_identity(nc, identity[:])
@@ -60,16 +59,13 @@ def tile_openpangusinkattention_kernel(tc, table, w, x, offs, out):
                 start=True,
                 stop=True,
             )
-        cos = cs[:, 0, :].unsqueeze(1).to_broadcast([P, GH, N])
-        sin = cs[:, 1, :].unsqueeze(1).to_broadcast([P, GH, N])
+        cs_heads = cs[:].unsqueeze(2).to_broadcast([P, 2, GH, N])
 
         for g in range(GROUPS):
             heads = slice(g * GH, (g + 1) * GH)
-            by_cos = held.tile([P, GH, N], F32, name=f"by_cos{g}")
-            by_sin = held.tile([P, GH, N], F32, name=f"by_sin{g}")
+            products = held.tile([P, 2, GH, N], F32, name=f"products{g}")
             rotated = held.tile([P, GH, N], F32, name=f"rotated{g}")
-            nc.vector.tensor_tensor(by_cos[:], x_same[g][:], cos, MULT)
-            nc.vector.tensor_tensor(by_sin[:], x_swap[g][:], sin, MULT)
-            nc.vector.tensor_tensor(rotated[:], by_cos[:], by_sin[:], ADD)
+            nc.vector.tensor_tensor(products[:], x_pair[g][:], cs_heads, MULT)
+            nc.vector.tensor_tensor(rotated[:], products[:, 0], products[:, 1], ADD)
             queue = nc.sync if g % 2 == 0 else nc.scalar
             queue.dma_start(out_heads[:, heads, :], rotated[:])

@@ -7,8 +7,7 @@ N = 64
 NH = 6
 HALF = 64
 BLOCKS = S // P
-GROUPS = 2
-GH = NH // GROUPS
+GH = NH // 2
 
 BF16, F32, U16 = mybir.dt.bfloat16, mybir.dt.float32, mybir.dt.uint16
 MULT, ADD = mybir.AluOpType.mult, mybir.AluOpType.add
@@ -18,8 +17,8 @@ FLOPS = 2 * P * 2 * P * N
 
 def tile_openpangusinkattention_kernel(tc, table, w, x, offs, out):
     nc = tc.nc
-    x_heads = x.rearrange("(h e) j -> e h j", e=P)
-    out_heads = out.rearrange("(h e) j -> e h j", e=P)
+    x_pairs = x.rearrange("(g h k i) j -> g i h k j", g=2, h=GH, k=2)
+    out_pairs = out.rearrange("(g h k i) j -> g k i h j", g=2, h=GH, k=2)
     with (
         tc.tile_pool(name="held", bufs=1) as held,
         tc.psum_pool(name="psum", bufs=1) as psum,
@@ -34,15 +33,18 @@ def tile_openpangusinkattention_kernel(tc, table, w, x, offs, out):
         weights = held.tile([P, 2 * P], BF16, name="weights")
         nc.scalar.dma_start(weights[:], w)
 
-        x_pair = [held.tile([P, 2, GH, N], F32, name=f"x_pair{g}") for g in range(GROUPS)]
-        for g in range(GROUPS):
-            heads = slice(g * GH, (g + 1) * GH)
-            nc.scalar.dma_start(x_pair[g][:, 0], x_heads[:, heads, :])
-            nc.sync.dma_start(x_pair[g][0:HALF, 1], x_heads[HALF:P, heads, :])
-            nc.sync.dma_start(x_pair[g][HALF:P, 1], x_heads[0:HALF, heads, :])
+        x_both = held.tile([P, GH, 2, N], F32, name="x_both")
+        nc.sync.dma_start(x_both[0:HALF], x_pairs[0])
+        nc.scalar.dma_start(x_both[HALF:P], x_pairs[1])
 
         identity = held.tile([P, P], BF16, name="identity")
         make_identity(nc, identity[:])
+
+        sign = held.tile([P, 2], F32, name="sign")
+        nc.vector.memset(sign[0:HALF, 0:1], 1.0)
+        nc.vector.memset(sign[HALF:P, 0:1], -1.0)
+        nc.vector.memset(sign[0:HALF, 1:2], -1.0)
+        nc.vector.memset(sign[HALF:P, 1:2], 1.0)
 
         flipped = psum.tile([P, S], BF16, name="flipped")
         for b in range(BLOCKS):
@@ -51,21 +53,27 @@ def tile_openpangusinkattention_kernel(tc, table, w, x, offs, out):
         nc.vector.tensor_copy(window[:], flipped[:])
 
         cs = psum.tile([P, 2, N], F32, name="cs")
-        for k in range(2):
+        for c in range(2):
             nc.tensor.matmul(
-                cs[:, k, :],
-                weights[:, k * P : (k + 1) * P],
+                cs[:, c, :],
+                weights[:, c * P : (c + 1) * P],
                 window[:].indirect(offsets[:]),
                 start=True,
                 stop=True,
             )
-        cs_heads = cs[:].unsqueeze(2).to_broadcast([P, 2, GH, N])
 
-        for g in range(GROUPS):
-            heads = slice(g * GH, (g + 1) * GH)
-            products = held.tile([P, 2, GH, N], F32, name=f"products{g}")
-            rotated = held.tile([P, GH, N], F32, name=f"rotated{g}")
-            nc.vector.tensor_tensor(products[:], x_pair[g][:], cs_heads, MULT)
-            nc.vector.tensor_tensor(rotated[:], products[:, 0], products[:, 1], ADD)
-            queue = nc.sync if g % 2 == 0 else nc.scalar
-            queue.dma_start(out_heads[:, heads, :], rotated[:])
+        by_cos = held.tile([P, GH, 2, N], F32, name="by_cos")
+        cos = cs[:, 0, :].unsqueeze(1).unsqueeze(1).to_broadcast([P, GH, 2, N])
+        nc.vector.tensor_tensor(by_cos[:], x_both[:], cos, MULT)
+        sin = cs[:, 1, :].unsqueeze(1).to_broadcast([P, GH, N])
+        by_sin = [held.tile([P, GH, N], F32, name=f"by_sin{k}") for k in range(2)]
+        for k in range(2):
+            nc.vector.tensor_tensor(by_sin[k][:], x_both[:, :, 1 - k, :], sin, MULT)
+
+        for k in range(2):
+            rotated = held.tile([P, GH, N], F32, name=f"rotated{k}")
+            nc.vector.scalar_tensor_tensor(
+                rotated[:], by_sin[k][:], sign[:, k : k + 1], by_cos[:, :, k, :], op0=MULT, op1=ADD
+            )
+            nc.sync.dma_start(out_pairs[0, k], rotated[0:HALF])
+            nc.scalar.dma_start(out_pairs[1, k], rotated[HALF:P])

@@ -46,16 +46,17 @@ def tile_openpangusinkattention_kernel(tc, table, w, x, offs, out):
         nc.vector.memset(sign[0:HALF, 1:2], -1.0)
         nc.vector.memset(sign[HALF:P, 1:2], 1.0)
 
-        flipped = psum.tile([P, S], BF16, name="flipped")
-        for b in range(BLOCKS):
-            nc.tensor.transpose(flipped[:, b * P : (b + 1) * P], rows[b][:], identity[:])
         window = held.tile([P, S], BF16, name="window")
-        nc.vector.tensor_copy(window[:], flipped[:])
+        for half in range(2):
+            flipped = psum.tile([P, 2 * P], BF16, name=f"flipped{half}")
+            for b in range(2):
+                nc.tensor.transpose(flipped[:, b * P : (b + 1) * P], rows[2 * half + b][:], identity[:])
+            nc.vector.tensor_copy(window[:, half * 2 * P : (half + 1) * 2 * P], flipped[:])
 
-        cs = psum.tile([P, 2, N], F32, name="cs")
+        cs = [psum.tile([P, N], F32, name=f"cs{c}") for c in range(2)]
         for c in range(2):
             nc.tensor.matmul(
-                cs[:, c, :],
+                cs[c][:],
                 weights[:, c * P : (c + 1) * P],
                 window[:].indirect(offsets[:]),
                 start=True,
@@ -63,9 +64,9 @@ def tile_openpangusinkattention_kernel(tc, table, w, x, offs, out):
             )
 
         by_cos = held.tile([P, GH, 2, N], F32, name="by_cos")
-        cos = cs[:, 0, :].unsqueeze(1).unsqueeze(1).to_broadcast([P, GH, 2, N])
+        cos = cs[0][:].unsqueeze(1).unsqueeze(1).to_broadcast([P, GH, 2, N])
         nc.vector.tensor_tensor(by_cos[:], x_both[:], cos, MULT)
-        sin = cs[:, 1, :].unsqueeze(1).to_broadcast([P, GH, N])
+        sin = cs[1][:].unsqueeze(1).to_broadcast([P, GH, N])
         by_sin = [held.tile([P, GH, N], F32, name=f"by_sin{k}") for k in range(2)]
         for k in range(2):
             nc.vector.tensor_tensor(by_sin[k][:], x_both[:, :, 1 - k, :], sin, MULT)

@@ -25,7 +25,7 @@ def tile_openpangusinkattention_kernel(tc, table, w, x, offs, out):
     ):
         rows = [held.tile([P, P], BF16, name=f"rows{b}") for b in range(BLOCKS)]
         for b in range(BLOCKS):
-            queue = nc.sync if b % 2 == 0 else nc.scalar
+            queue = nc.sync if b < BLOCKS // 2 else nc.scalar
             queue.dma_start(rows[b][:], table[b * P : (b + 1) * P, :])
 
         offsets = held.tile([P, N // 16], U16, name="offsets")

import concourse.mybir as mybir
from concourse.masks import make_identity

P = 128
S = 512
N = 64
NH = 6
HALF = 64
BLOCKS = S // P
GH = NH // 2

BF16, F32, U16 = mybir.dt.bfloat16, mybir.dt.float32, mybir.dt.uint16
MULT, ADD = mybir.AluOpType.mult, mybir.AluOpType.add

FLOPS = 2 * P * 2 * P * N


def tile_openpangusinkattention_kernel(tc, table, w, x, offs, out):
    nc = tc.nc
    x_pairs = x.rearrange("(g h k i) j -> g i h k j", g=2, h=GH, k=2)
    out_pairs = out.rearrange("(g h k i) j -> g k i h j", g=2, h=GH, k=2)
    with (
        tc.tile_pool(name="held", bufs=1) as held,
        tc.psum_pool(name="psum", bufs=1) as psum,
    ):
        rows = [held.tile([P, P], BF16, name=f"rows{b}") for b in range(BLOCKS)]
        for b in range(BLOCKS):
            queue = nc.sync if b < BLOCKS // 2 else nc.scalar
            queue.dma_start(rows[b][:], table[b * P : (b + 1) * P, :])

        offsets = held.tile([P, N // 16], U16, name="offsets")
        nc.sync.dma_start(offsets[:], offs)
        weights = held.tile([P, 2 * P], BF16, name="weights")
        nc.scalar.dma_start(weights[:], w)

        x_both = held.tile([P, GH, 2, N], F32, name="x_both")
        nc.sync.dma_start(x_both[0:HALF], x_pairs[0])
        nc.scalar.dma_start(x_both[HALF:P], x_pairs[1])

        identity = held.tile([P, P], BF16, name="identity")
        make_identity(nc, identity[:])

        sign = held.tile([P, 2], F32, name="sign")
        nc.vector.memset(sign[0:HALF, 0:1], 1.0)
        nc.vector.memset(sign[HALF:P, 0:1], -1.0)
        nc.vector.memset(sign[0:HALF, 1:2], -1.0)
        nc.vector.memset(sign[HALF:P, 1:2], 1.0)

        window = held.tile([P, S], BF16, name="window")
        for half in range(2):
            flipped = psum.tile([P, 2 * P], BF16, name=f"flipped{half}")
            for b in range(2):
                nc.tensor.transpose(flipped[:, b * P : (b + 1) * P], rows[2 * half + b][:], identity[:])
            nc.vector.tensor_copy(window[:, half * 2 * P : (half + 1) * 2 * P], flipped[:])

        cs = [psum.tile([P, N], F32, name=f"cs{c}") for c in range(2)]
        for c in range(2):
            nc.tensor.matmul(
                cs[c][:],
                weights[:, c * P : (c + 1) * P],
                window[:].indirect(offsets[:]),
                start=True,
                stop=True,
            )

        by_cos = held.tile([P, GH, 2, N], F32, name="by_cos")
        cos = cs[0][:].unsqueeze(1).unsqueeze(1).to_broadcast([P, GH, 2, N])
        nc.vector.tensor_tensor(by_cos[:], x_both[:], cos, MULT)
        sin = cs[1][:].unsqueeze(1).to_broadcast([P, GH, N])
        by_sin = [held.tile([P, GH, N], F32, name=f"by_sin{k}") for k in range(2)]
        for k in range(2):
            nc.vector.tensor_tensor(by_sin[k][:], x_both[:, :, 1 - k, :], sin, MULT)

        for k in range(2):
            rotated = held.tile([P, GH, N], F32, name=f"rotated{k}")
            nc.vector.scalar_tensor_tensor(
                rotated[:], by_sin[k][:], sign[:, k : k + 1], by_cos[:, :, k, :], op0=MULT, op1=ADD
            )
            nc.sync.dma_start(out_pairs[0, k], rotated[0:HALF])
            nc.scalar.dma_start(out_pairs[1, k], rotated[HALF:P])
